import numpy as np
import ml_dtypes


def mxq(x, axis, fmt="e4m3"):
    dtype, down = {"e4m3": (ml_dtypes.float8_e4m3fn, 7), "e5m2": (ml_dtypes.float8_e5m2, 14)}[fmt]
    v = np.moveaxis(np.asarray(x, np.float32).astype(ml_dtypes.bfloat16).astype(np.float64), axis, -1)
    blocks = v.reshape(v.shape[:-1] + (-1, 32))
    amax = np.abs(blocks).max(-1, keepdims=True)
    byte = np.maximum(np.where(amax > 0, np.frexp(amax)[1] - 1 + 127, 0) - down, 1)
    scale = np.exp2(byte - 127.0)
    codes = (blocks / scale).astype(np.float32).astype(dtype).astype(np.float64)
    return np.moveaxis((codes * scale).reshape(v.shape), -1, axis)


WIDE = False


def mx_kscale(k):
    if not WIDE:
        return np.ones(k)
    levels = np.array([10, -10, 5, -5, 0])
    if k % 512:
        return np.exp2(np.random.permutation(np.resize(levels, k // 32))).repeat(32)
    a = np.empty((k // 512, 16))
    for p in range(k // 512):
        a[p, :8] = np.random.permutation(np.resize(levels, 8))
        for g in range(8):
            far = levels[np.abs(levels - a[p, g]) >= 10]
            a[p, g + 8] = far[np.random.randint(len(far))]
    return np.exp2(a.ravel()).repeat(32)


BF16 = ml_dtypes.bfloat16


def bf(x):
    return np.asarray(x, np.float32).astype(BF16)


def f64(x):
    return np.asarray(x).astype(np.float64)


B, P0, P1, P2, K0, K1, K2 = 4096, 512, 512, 512, 128, 128, 128
PT = P0 + P1 + P2
KT = K0 + K1 + K2
CLIP0 = 1.0


def clip_rows(mat, clip):
    norms = np.sqrt(np.sum(mat * mat, axis=1, keepdims=True))
    scale = np.minimum(clip / norms, 1.0)
    return mat * scale


def setup_inputs():
    s0, s1, s2 = mx_kscale(P0), mx_kscale(P1), mx_kscale(P2)
    r = np.exp2(np.random.uniform(-2.0, 2.0, (B, 1))) / (KT * PT) ** 0.25
    return {"target_grad": bf(np.random.standard_normal((B, PT)) * r * np.concatenate([s0, s1, s2])),
            "bases0": bf(np.random.standard_normal((P0, K0)) / np.sqrt(P0) / s0[:, None]),
            "bases1": bf(np.random.standard_normal((P1, K1)) / np.sqrt(P1) / s1[:, None]),
            "bases2": bf(np.random.standard_normal((P2, K2)) / np.sqrt(P2) / s2[:, None])}


def reference(target_grad, bases0, bases1, bases2):
    g = f64(target_grad)
    embeddings = []
    offset = 0
    for b in (f64(bases0), f64(bases1), f64(bases2)):
        num_p = b.shape[0]
        embeddings.append(mxq(g[:, offset:offset + num_p], 1, "e4m3") @ mxq(b, 0, "e4m3"))
        offset += num_p
    embedding = np.concatenate(embeddings, axis=1)
    avg_clipped_embedding = np.sum(clip_rows(embedding, CLIP0), axis=0) / B
    return embedding, avg_clipped_embedding

@@ -1,0 +1,209 @@
+from contextlib import ExitStack
+
+import concourse.mybir as mybir
+from concourse.masks import make_identity
+
+F32 = mybir.dt.float32
+BF16 = mybir.dt.bfloat16
+U32 = mybir.dt.uint32
+U8 = mybir.dt.uint8
+FP8X4 = mybir.dt.float8_e4m3fn_x4
+ACT = mybir.ActivationFunctionType
+ALU = mybir.AluOpType
+AXIS = mybir.AxisListType
+
+P = 128
+PACK = 4
+HALVES = 2
+BATCH = 4096
+GROUPS = 3
+K_GROUP = P * PACK
+EMB = 128
+EMB_ALL = GROUPS * EMB
+TILES = 2
+UNITS = BATCH // (TILES * P)
+CLIP = 1.0
+SCALAR_BANKS = 3
+OF_BANKS = 8
+
+FLOPS = 2 * BATCH * GROUPS * K_GROUP * EMB
+
+
+def tile_gep_pa_t_kernel(tc, target_grad, bases0, bases1, bases2, out_0, out_1):
+    nc = tc.nc
+    bases = [bases0, bases1, bases2]
+
+    grad_pieces = target_grad.rearrange("(u p t) (g k) -> u g p t k", p=P, t=TILES, g=GROUPS)
+    emb_units = out_0.rearrange("(u p t) j -> u p (t j)", p=P, t=TILES)
+
+    with ExitStack() as ctx:
+        ctx.enter_context(tc.manual_schedule())
+        const = ctx.enter_context(tc.tile_pool(name="const", bufs=1))
+        grads = ctx.enter_context(tc.tile_pool(name="grads", bufs=UNITS))
+        stage = ctx.enter_context(tc.tile_pool(name="stage", bufs=3))
+        embs = ctx.enter_context(tc.tile_pool(name="embs", bufs=UNITS))
+        small = ctx.enter_context(tc.tile_pool(name="small", bufs=6))
+        flipped_psum = ctx.enter_context(tc.psum_pool(name="flipped_psum", bufs=4))
+        emb_psum = ctx.enter_context(tc.psum_pool(name="emb_psum", bufs=3))
+        mean_psum = ctx.enter_context(tc.psum_pool(name="mean_psum", bufs=1))
+
+        grad_sb = []
+        for u in range(UNITS):
+            grad = grads.tile([P, GROUPS, TILES, K_GROUP], BF16)
+            for g in range(GROUPS):
+                nc.sync.dma_start(out=grad[:, g], in_=grad_pieces[u, g])
+            grad_sb.append(grad)
+
+        base_rows = const.tile([P, GROUPS, PACK, EMB], BF16)
+        for g in range(GROUPS):
+            nc.scalar.dma_start(
+                out=base_rows[:, g],
+                in_=bases[g].rearrange("(p t) c -> p t c", t=PACK),
+            )
+
+        identity = const.tile([P, P], F32)
+        make_identity(nc, identity[:])
+        minus_half = const.tile([P, TILES], F32)
+        nc.gpsimd.memset(minus_half[:], -0.5)
+        column_sums = const.tile([P, P], F32)
+        nc.vector.memset(column_sums[:], 0.0)
+        weighted = mean_psum.tile([P, GROUPS, P], F32)
+
+        base_grouped = const.tile([P, GROUPS, EMB, PACK], BF16, align_bytes=64)
+        nc.vector.tensor_copy(
+            out=base_grouped[:], in_=base_rows[:].rearrange("p g t c -> p g c t")
+        )
+        base_codes = const.tile([P, GROUPS, EMB], U32, align_bytes=64)
+        base_scales = const.tile([P, GROUPS, EMB], U8, align_bytes=64)
+        for g in range(GROUPS):
+            nc.vector.quantize_mx(
+                out=base_codes[:, g, :].bitcast(FP8X4),
+                scales=base_scales[:, g, :],
+                in_=base_grouped[:, g].rearrange("p c t -> p (c t)"),
+            )
+
+        grouped_sb = {}
+        codes_sb = {}
+        scales_sb = {}
+        emb_sb = {}
+        square_sum_sb = {}
+        factor_sb = {}
+        scaled_sb = {}
+
+        def flip_and_regroup(u):
+            grouped = stage.tile([P, GROUPS, TILES * P * PACK], BF16, align_bytes=64)
+            grouped_sb[u] = grouped
+            for g in range(GROUPS):
+                flipped = flipped_psum.tile([P, TILES, HALVES, P], F32)
+                for t in range(TILES):
+                    words = grad_sb[u][:, g, t, :].bitcast(F32)
+                    for h in range(HALVES):
+                        nc.tensor.transpose(
+                            flipped[:, t, h, :], words[:, h : HALVES * P : HALVES], identity[:]
+                        )
+                bank = u * GROUPS + g
+                to_scalar = (bank * SCALAR_BANKS) % OF_BANKS < SCALAR_BANKS
+                copy = nc.scalar.copy if to_scalar else nc.vector.tensor_copy
+                copy(
+                    out=grouped[:, g, :]
+                    .bitcast(F32)
+                    .rearrange("p (t b h) -> p t b h", t=TILES, h=HALVES),
+                    in_=flipped[:].rearrange("p t h b -> p t b h"),
+                )
+
+        def quantise(u):
+            codes = stage.tile([P, GROUPS, TILES * P], U32, align_bytes=64)
+            scales = stage.tile([P, GROUPS, TILES * P], U8, align_bytes=64)
+            codes_sb[u] = codes
+            scales_sb[u] = scales
+            for groups in (slice(0, 2), slice(2, 3)):
+                nc.vector.quantize_mx(
+                    out=codes[:, groups, :].rearrange("p g c -> p (g c)").bitcast(FP8X4),
+                    scales=scales[:, groups, :].rearrange("p g c -> p (g c)"),
+                    in_=grouped_sb[u][:, groups, :].rearrange("p g c -> p (g c)"),
+                )
+
+        def project(u):
+            emb = embs.tile([P, TILES, EMB_ALL], F32)
+            emb_sb[u] = emb
+            square_sum = small.tile([P, TILES], F32)
+            square_sum_sb[u] = square_sum
+            accs = []
+            for t in range(TILES):
+                rows = slice(t * P, (t + 1) * P)
+                acc = emb_psum.tile([P, EMB_ALL], F32)
+                accs.append(acc)
+                for g in range(GROUPS):
+                    nc.tensor.matmul_mx(
+                        out=acc[:, g * EMB : (g + 1) * EMB],
+                        lhsT=codes_sb[u][:, g, rows].bitcast(FP8X4),
+                        lhsT_scale=scales_sb[u][:, g, rows],
+                        rhs=base_codes[:, g, :].bitcast(FP8X4),
+                        rhs_scale=base_scales[:, g, :],
+                        start=True,
+                        stop=True,
+                    )
+            for t in range(TILES):
+                squares = stage.tile([P, EMB_ALL], F32)
+                nc.scalar.activation(
+                    out=squares[:],
+                    in_=accs[t][:],
+                    func=ACT.Square,
+                    accum_out=square_sum[:, t : t + 1],
+                )
+            for t in range(TILES):
+                nc.scalar.copy(out=emb[:, t, :], in_=accs[t][:])
+            nc.sync.dma_start(out=emb_units[u], in_=emb[:].rearrange("p t j -> p (t j)"))
+
+        def clip_factor(u):
+            floored = small.tile([P, TILES], F32)
+            nc.gpsimd.tensor_scalar_max(floored[:], square_sum_sb[u][:], CLIP * CLIP)
+            factor = small.tile([P, TILES], F32)
+            factor_sb[u] = factor
+            nc.gpsimd.tensor_tensor(out=factor[:], in0=floored[:], in1=minus_half[:], op=ALU.pow)
+
+        def weigh(u):
+            scaled = stage.tile([P, TILES, EMB_ALL], F32)
+            scaled_sb[u] = scaled
+            for t in range(TILES):
+                nc.vector.tensor_scalar_mul(
+                    scaled[:, t, :], emb_sb[u][:, t, :], factor_sb[u][:, t : t + 1]
+                )
+
+        def add_up(u):
+            for t in range(TILES):
+                for g in range(GROUPS):
+                    nc.tensor.matmul(
+                        out=weighted[:, g, :],
+                        lhsT=scaled_sb[u][:, t, g * EMB : (g + 1) * EMB],
+                        rhs=identity[:],
+                        is_transpose=True,
+                        start=(u == 0 and t == 0 and g == 0),
+                        stop=(u == UNITS - 1 and t == TILES - 1 and g == GROUPS - 1),
+                    )
+
+        for step in range(UNITS + 3):
+            if 0 <= step - 1 < UNITS:
+                quantise(step - 1)
+            if step < UNITS:
+                flip_and_regroup(step)
+            if 0 <= step - 3 < UNITS:
+                add_up(step - 3)
+            if 0 <= step - 1 < UNITS:
+                project(step - 1)
+                clip_factor(step - 1)
+            if 0 <= step - 2 < UNITS:
+                weigh(step - 2)
+
+        nc.vector.tensor_reduce(
+            out=column_sums[:, 0:GROUPS], in_=weighted[:], axis=AXIS.X, op=ALU.add
+        )
+        sums_flipped = flipped_psum.tile([P, TILES, HALVES, P], F32, tag="flipped")
+        nc.tensor.transpose(sums_flipped[:, 0, 0, :], column_sums[:], identity[:])
+        avg = const.tile([P, EMB], F32)
+        nc.scalar.activation(
+            out=avg[:], in_=sums_flipped[:, 0, 0, :], func=ACT.Copy, scale=CLIP / BATCH
+        )
+        nc.sync.dma_start(
+            out=out_1.rearrange("(g j) -> g j", g=GROUPS), in_=avg[0:GROUPS, :]
+        )

@@ -63,8 +63,6 @@ def tile_gep_pa_t_kernel(tc, target_grad, bases0, bases1, bases2, out_0, out_1):
 
         identity = const.tile([P, P], F32)
         make_identity(nc, identity[:])
-        minus_half = const.tile([P, TILES], F32)
-        nc.gpsimd.memset(minus_half[:], -0.5)
         column_sums = const.tile([P, P], F32)
         nc.vector.memset(column_sums[:], 0.0)
         weighted = mean_psum.tile([P, GROUPS, P], F32)
@@ -87,6 +85,8 @@ def tile_gep_pa_t_kernel(tc, target_grad, bases0, bases1, bases2, out_0, out_1):
         scales_sb = {}
         emb_sb = {}
         square_sum_sb = {}
+        norm_sb = {}
+        floored_sb = {}
         factor_sb = {}
         scaled_sb = {}
 
@@ -153,14 +153,20 @@ def tile_gep_pa_t_kernel(tc, target_grad, bases0, bases1, bases2, out_0, out_1):
                 )
             for t in range(TILES):
                 nc.scalar.copy(out=emb[:, t, :], in_=accs[t][:])
+            norm = small.tile([P, TILES], F32)
+            norm_sb[u] = norm
+            nc.scalar.activation(out=norm[:], in_=square_sum[:], func=ACT.Sqrt)
             nc.sync.dma_start(out=emb_units[u], in_=emb[:].rearrange("p t j -> p (t j)"))
 
-        def clip_factor(u):
+        def floor_norm(u):
             floored = small.tile([P, TILES], F32)
-            nc.gpsimd.tensor_scalar_max(floored[:], square_sum_sb[u][:], CLIP * CLIP)
+            floored_sb[u] = floored
+            nc.vector.tensor_scalar_max(floored[:], norm_sb[u][:], CLIP)
+
+        def clip_factor(u):
             factor = small.tile([P, TILES], F32)
             factor_sb[u] = factor
-            nc.gpsimd.tensor_tensor(out=factor[:], in0=floored[:], in1=minus_half[:], op=ALU.pow)
+            nc.vector.reciprocal(out=factor[:], in_=floored_sb[u][:])
 
         def weigh(u):
             scaled = stage.tile([P, TILES, EMB_ALL], F32)
@@ -185,13 +191,16 @@ def tile_gep_pa_t_kernel(tc, target_grad, bases0, bases1, bases2, out_0, out_1):
         for step in range(UNITS + 3):
             if 0 <= step - 1 < UNITS:
                 quantise(step - 1)
+            if 0 <= step - 2 < UNITS:
+                floor_norm(step - 2)
             if step < UNITS:
                 flip_and_regroup(step)
+            if 0 <= step - 2 < UNITS:
+                clip_factor(step - 2)
             if 0 <= step - 3 < UNITS:
                 add_up(step - 3)
             if 0 <= step - 1 < UNITS:
                 project(step - 1)
-                clip_factor(step - 1)
             if 0 <= step - 2 < UNITS:
                 weigh(step - 2)
 

@@ -22,9 +22,10 @@ EMB = 128
 EMB_ALL = GROUPS * EMB
 TILES = 2
 UNITS = BATCH // (TILES * P)
+BATCHED = 2
 CLIP = 1.0
-SCALAR_BANKS = 3
-OF_BANKS = 8
+SCALAR_BANKS = 7
+OF_BANKS = 16
 
 FLOPS = 2 * BATCH * GROUPS * K_GROUP * EMB
 
@@ -33,7 +34,7 @@ def tile_gep_pa_t_kernel(tc, target_grad, bases0, bases1, bases2, out_0, out_1):
     nc = tc.nc
     bases = [bases0, bases1, bases2]
 
-    grad_pieces = target_grad.rearrange("(u p t) (g k) -> u g p t k", p=P, t=TILES, g=GROUPS)
+    grad_units = target_grad.rearrange("(u p t) (g k) -> u p t g k", p=P, t=TILES, g=GROUPS)
     emb_units = out_0.rearrange("(u p t) j -> u p (t j)", p=P, t=TILES)
 
     with ExitStack() as ctx:
@@ -49,9 +50,9 @@ def tile_gep_pa_t_kernel(tc, target_grad, bases0, bases1, bases2, out_0, out_1):
 
         grad_sb = []
         for u in range(UNITS):
-            grad = grads.tile([P, GROUPS, TILES, K_GROUP], BF16)
-            for g in range(GROUPS):
-                nc.sync.dma_start(out=grad[:, g], in_=grad_pieces[u, g])
+            grad = grads.tile([P, TILES, GROUPS, K_GROUP], BF16)
+            for groups in [slice(g, g + 1) for g in range(GROUPS)] if u == 0 else [slice(0, GROUPS)]:
+                nc.sync.dma_start(out=grad[:, :, groups], in_=grad_units[u, :, :, groups])
             grad_sb.append(grad)
 
         base_rows = const.tile([P, GROUPS, PACK, EMB], BF16)
@@ -63,6 +64,9 @@ def tile_gep_pa_t_kernel(tc, target_grad, bases0, bases1, bases2, out_0, out_1):
 
         identity = const.tile([P, P], F32)
         make_identity(nc, identity[:])
+        root = const.tile([P, 1], F32)
+        nc.gpsimd.memset(root[:], 1.0)
+        nc.scalar.activation(out=root[:], in_=root[:], func=ACT.Sqrt)
         column_sums = const.tile([P, P], F32)
         nc.vector.memset(column_sums[:], 0.0)
         weighted = mean_psum.tile([P, GROUPS, P], F32)
@@ -96,7 +100,7 @@ def tile_gep_pa_t_kernel(tc, target_grad, bases0, bases1, bases2, out_0, out_1):
             for g in range(GROUPS):
                 flipped = flipped_psum.tile([P, TILES, HALVES, P], F32)
                 for t in range(TILES):
-                    words = grad_sb[u][:, g, t, :].bitcast(F32)
+                    words = grad_sb[u][:, t, g, :].bitcast(F32)
                     for h in range(HALVES):
                         nc.tensor.transpose(
                             flipped[:, t, h, :], words[:, h : HALVES * P : HALVES], identity[:]
@@ -126,8 +130,9 @@ def tile_gep_pa_t_kernel(tc, target_grad, bases0, bases1, bases2, out_0, out_1):
         def project(u):
             emb = embs.tile([P, TILES, EMB_ALL], F32)
             emb_sb[u] = emb
-            square_sum = small.tile([P, TILES], F32)
-            square_sum_sb[u] = square_sum
+            if u % BATCHED == 0:
+                square_sum_sb[u // BATCHED] = small.tile([P, BATCHED, TILES], F32, name="square_sum")
+            square_sum = square_sum_sb[u // BATCHED][:, u % BATCHED, :]
             accs = []
             for t in range(TILES):
                 rows = slice(t * P, (t + 1) * P)
@@ -153,27 +158,30 @@ def tile_gep_pa_t_kernel(tc, target_grad, bases0, bases1, bases2, out_0, out_1):
                 )
             for t in range(TILES):
                 nc.scalar.copy(out=emb[:, t, :], in_=accs[t][:])
-            norm = small.tile([P, TILES], F32)
-            norm_sb[u] = norm
-            nc.scalar.activation(out=norm[:], in_=square_sum[:], func=ACT.Sqrt)
             nc.sync.dma_start(out=emb_units[u], in_=emb[:].rearrange("p t j -> p (t j)"))
+            if u % BATCHED == BATCHED - 1:
+                norm = small.tile([P, BATCHED, TILES], F32)
+                norm_sb[u // BATCHED] = norm
+                nc.scalar.activation(out=norm[:], in_=square_sum_sb[u // BATCHED][:], func=ACT.Sqrt)
 
         def floor_norm(u):
-            floored = small.tile([P, TILES], F32)
-            floored_sb[u] = floored
-            nc.vector.tensor_scalar_max(floored[:], norm_sb[u][:], CLIP)
+            if u % BATCHED == BATCHED - 1:
+                floored = small.tile([P, BATCHED, TILES], F32)
+                floored_sb[u // BATCHED] = floored
+                nc.vector.tensor_scalar_max(floored[:], norm_sb[u // BATCHED][:], CLIP)
 
         def clip_factor(u):
-            factor = small.tile([P, TILES], F32)
-            factor_sb[u] = factor
-            nc.vector.reciprocal(out=factor[:], in_=floored_sb[u][:])
+            if u % BATCHED == BATCHED - 1:
+                factor = small.tile([P, BATCHED, TILES], F32)
+                factor_sb[u // BATCHED] = factor
+                nc.vector.reciprocal(out=factor[:], in_=floored_sb[u // BATCHED][:])
 
         def weigh(u):
             scaled = stage.tile([P, TILES, EMB_ALL], F32)
             scaled_sb[u] = scaled
             for t in range(TILES):
                 nc.vector.tensor_scalar_mul(
-                    scaled[:, t, :], emb_sb[u][:, t, :], factor_sb[u][:, t : t + 1]
+                    scaled[:, t, :], emb_sb[u][:, t, :], factor_sb[u // BATCHED][:, u % BATCHED, t : t + 1]
                 )
 
         def add_up(u):
@@ -188,21 +196,21 @@ def tile_gep_pa_t_kernel(tc, target_grad, bases0, bases1, bases2, out_0, out_1):
                         stop=(u == UNITS - 1 and t == TILES - 1 and g == GROUPS - 1),
                     )
 
-        for step in range(UNITS + 3):
+        for step in range(UNITS + 5):
             if 0 <= step - 1 < UNITS:
                 quantise(step - 1)
-            if 0 <= step - 2 < UNITS:
-                floor_norm(step - 2)
+            if 0 <= step - 3 < UNITS:
+                floor_norm(step - 3)
             if step < UNITS:
                 flip_and_regroup(step)
-            if 0 <= step - 2 < UNITS:
-                clip_factor(step - 2)
             if 0 <= step - 3 < UNITS:
-                add_up(step - 3)
+                clip_factor(step - 3)
+            if 0 <= step - 5 < UNITS:
+                add_up(step - 5)
             if 0 <= step - 1 < UNITS:
                 project(step - 1)
-            if 0 <= step - 2 < UNITS:
-                weigh(step - 2)
+            if 0 <= step - 4 < UNITS:
+                weigh(step - 4)
 
         nc.vector.tensor_reduce(
             out=column_sums[:, 0:GROUPS], in_=weighted[:], axis=AXIS.X, op=ALU.add

@@ -24,6 +24,8 @@ TILES = 2
 UNITS = BATCH // (TILES * P)
 BATCHED = 2
 CLIP = 1.0
+WARM_COLUMNS = 512
+WARM_MATMULS = 5
 SCALAR_BANKS = 7
 OF_BANKS = 16
 
@@ -48,19 +50,25 @@ def tile_gep_pa_t_kernel(tc, target_grad, bases0, bases1, bases2, out_0, out_1):
         emb_psum = ctx.enter_context(tc.psum_pool(name="emb_psum", bufs=3))
         mean_psum = ctx.enter_context(tc.psum_pool(name="mean_psum", bufs=1))
 
+        base_rows = const.tile([P, GROUPS, PACK, EMB], BF16)
         grad_sb = []
         for u in range(UNITS):
+            if u == 1:
+                for g in range(GROUPS):
+                    nc.sync.dma_start(
+                        out=base_rows[:, g],
+                        in_=bases[g].rearrange("(p t) c -> p t c", t=PACK),
+                    )
             grad = grads.tile([P, TILES, GROUPS, K_GROUP], BF16)
             for groups in [slice(g, g + 1) for g in range(GROUPS)] if u == 0 else [slice(0, GROUPS)]:
                 nc.sync.dma_start(out=grad[:, :, groups], in_=grad_units[u, :, :, groups])
             grad_sb.append(grad)
 
-        base_rows = const.tile([P, GROUPS, PACK, EMB], BF16)
-        for g in range(GROUPS):
-            nc.scalar.dma_start(
-                out=base_rows[:, g],
-                in_=bases[g].rearrange("(p t) c -> p t c", t=PACK),
-            )
+        zeros = const.tile([P, WARM_COLUMNS], BF16)
+        nc.vector.memset(zeros[:], 0.0)
+        warm = emb_psum.tile([P, WARM_COLUMNS], F32, tag="acc")
+        for i in range(WARM_MATMULS):
+            nc.tensor.matmul(out=warm[:], lhsT=zeros[:, 0:P], rhs=zeros[:], start=True, stop=True)
 
         identity = const.tile([P, P], F32)
         make_identity(nc, identity[:])
@@ -72,17 +80,25 @@ def tile_gep_pa_t_kernel(tc, target_grad, bases0, bases1, bases2, out_0, out_1):
         weighted = mean_psum.tile([P, GROUPS, P], F32)
 
         base_grouped = const.tile([P, GROUPS, EMB, PACK], BF16, align_bytes=64)
-        nc.vector.tensor_copy(
-            out=base_grouped[:], in_=base_rows[:].rearrange("p g t c -> p g c t")
-        )
+        for g in range(GROUPS):
+            nc.gpsimd.tensor_scalar(
+                out=base_grouped[:, g],
+                in0=base_rows[:, g].rearrange("p t c -> p c t"),
+                scalar1=1.0,
+                scalar2=0.0,
+                op0=ALU.mult,
+                op1=ALU.add,
+            )
         base_codes = const.tile([P, GROUPS, EMB], U32, align_bytes=64)
         base_scales = const.tile([P, GROUPS, EMB], U8, align_bytes=64)
-        for g in range(GROUPS):
-            nc.vector.quantize_mx(
-                out=base_codes[:, g, :].bitcast(FP8X4),
-                scales=base_scales[:, g, :],
-                in_=base_grouped[:, g].rearrange("p c t -> p (c t)"),
-            )
+
+        def quantise_bases():
+            for g in range(GROUPS):
+                nc.vector.quantize_mx(
+                    out=base_codes[:, g, :].bitcast(FP8X4),
+                    scales=base_scales[:, g, :],
+                    in_=base_grouped[:, g].rearrange("p c t -> p (c t)"),
+                )
 
         grouped_sb = {}
         codes_sb = {}
@@ -156,13 +172,18 @@ def tile_gep_pa_t_kernel(tc, target_grad, bases0, bases1, bases2, out_0, out_1):
                     func=ACT.Square,
                     accum_out=square_sum[:, t : t + 1],
                 )
+            if u == UNITS - 1:
+                take_roots(u)
             for t in range(TILES):
                 nc.scalar.copy(out=emb[:, t, :], in_=accs[t][:])
             nc.sync.dma_start(out=emb_units[u], in_=emb[:].rearrange("p t j -> p (t j)"))
-            if u % BATCHED == BATCHED - 1:
-                norm = small.tile([P, BATCHED, TILES], F32)
-                norm_sb[u // BATCHED] = norm
-                nc.scalar.activation(out=norm[:], in_=square_sum_sb[u // BATCHED][:], func=ACT.Sqrt)
+            if u % BATCHED == BATCHED - 1 and u != UNITS - 1:
+                take_roots(u)
+
+        def take_roots(u):
+            norm = small.tile([P, BATCHED, TILES], F32)
+            norm_sb[u // BATCHED] = norm
+            nc.scalar.activation(out=norm[:], in_=square_sum_sb[u // BATCHED][:], func=ACT.Sqrt)
 
         def floor_norm(u):
             if u % BATCHED == BATCHED - 1:
@@ -197,6 +218,8 @@ def tile_gep_pa_t_kernel(tc, target_grad, bases0, bases1, bases2, out_0, out_1):
                     )
 
         for step in range(UNITS + 5):
+            if step == 1:
+                quantise_bases()
             if 0 <= step - 1 < UNITS:
                 quantise(step - 1)
             if 0 <= step - 3 < UNITS:
@@ -221,6 +244,6 @@ def tile_gep_pa_t_kernel(tc, target_grad, bases0, bases1, bases2, out_0, out_1):
         nc.scalar.activation(
             out=avg[:], in_=sums_flipped[:, 0, 0, :], func=ACT.Copy, scale=CLIP / BATCH
         )
-        nc.sync.dma_start(
+        nc.scalar.dma_start(
             out=out_1.rearrange("(g j) -> g j", g=GROUPS), in_=avg[0:GROUPS, :]
         )

@@ -22,7 +22,6 @@ EMB = 128
 EMB_ALL = GROUPS * EMB
 TILES = 2
 UNITS = BATCH // (TILES * P)
-BATCHED = 2
 CLIP = 1.0
 WARM_COLUMNS = 512
 WARM_MATMULS = 5
@@ -45,6 +44,7 @@ def tile_gep_pa_t_kernel(tc, target_grad, bases0, bases1, bases2, out_0, out_1):
         grads = ctx.enter_context(tc.tile_pool(name="grads", bufs=UNITS))
         stage = ctx.enter_context(tc.tile_pool(name="stage", bufs=3))
         embs = ctx.enter_context(tc.tile_pool(name="embs", bufs=UNITS))
+        scaled_pool = ctx.enter_context(tc.tile_pool(name="scaled_pool", bufs=5))
         small = ctx.enter_context(tc.tile_pool(name="small", bufs=6))
         flipped_psum = ctx.enter_context(tc.psum_pool(name="flipped_psum", bufs=4))
         emb_psum = ctx.enter_context(tc.psum_pool(name="emb_psum", bufs=3))
@@ -53,16 +53,21 @@ def tile_gep_pa_t_kernel(tc, target_grad, bases0, bases1, bases2, out_0, out_1):
         base_rows = const.tile([P, GROUPS, PACK, EMB], BF16)
         grad_sb = []
         for u in range(UNITS):
-            if u == 1:
+            if u == 2:
                 for g in range(GROUPS):
                     nc.sync.dma_start(
                         out=base_rows[:, g],
                         in_=bases[g].rearrange("(p t) c -> p t c", t=PACK),
                     )
-            grad = grads.tile([P, TILES, GROUPS, K_GROUP], BF16)
-            for groups in [slice(g, g + 1) for g in range(GROUPS)] if u == 0 else [slice(0, GROUPS)]:
-                nc.sync.dma_start(out=grad[:, :, groups], in_=grad_units[u, :, :, groups])
-            grad_sb.append(grad)
+            if u == 0:
+                grad = grads.tile([P, GROUPS, TILES, K_GROUP], BF16, tag="grad")
+                for g in range(GROUPS):
+                    nc.sync.dma_start(out=grad[:, g], in_=grad_units[u, :, :, g])
+                grad_sb.append(grad[:].rearrange("p g t k -> p t g k"))
+            else:
+                grad = grads.tile([P, TILES, GROUPS, K_GROUP], BF16, tag="grad")
+                nc.sync.dma_start(out=grad[:], in_=grad_units[u])
+                grad_sb.append(grad[:])
 
         zeros = const.tile([P, WARM_COLUMNS], BF16)
         nc.vector.memset(zeros[:], 0.0)
@@ -80,15 +85,20 @@ def tile_gep_pa_t_kernel(tc, target_grad, bases0, bases1, bases2, out_0, out_1):
         weighted = mean_psum.tile([P, GROUPS, P], F32)
 
         base_grouped = const.tile([P, GROUPS, EMB, PACK], BF16, align_bytes=64)
-        for g in range(GROUPS):
-            nc.gpsimd.tensor_scalar(
-                out=base_grouped[:, g],
-                in0=base_rows[:, g].rearrange("p t c -> p c t"),
-                scalar1=1.0,
-                scalar2=0.0,
-                op0=ALU.mult,
-                op1=ALU.add,
-            )
+        base_columns = base_rows[:].rearrange("p g t c -> p g c t")
+        nc.gpsimd.tensor_scalar(
+            out=base_grouped[:, 0],
+            in0=base_columns[:, 0],
+            scalar1=1.0,
+            scalar2=0.0,
+            op0=ALU.mult,
+            op1=ALU.add,
+        )
+
+        def regroup_bases():
+            nc.scalar.copy(out=base_grouped[:, 1], in_=base_columns[:, 1])
+            nc.vector.tensor_copy(out=base_grouped[:, 2], in_=base_columns[:, 2])
+
         base_codes = const.tile([P, GROUPS, EMB], U32, align_bytes=64)
         base_scales = const.tile([P, GROUPS, EMB], U8, align_bytes=64)
 
@@ -146,9 +156,10 @@ def tile_gep_pa_t_kernel(tc, target_grad, bases0, bases1, bases2, out_0, out_1):
         def project(u):
             emb = embs.tile([P, TILES, EMB_ALL], F32)
             emb_sb[u] = emb
-            if u % BATCHED == 0:
-                square_sum_sb[u // BATCHED] = small.tile([P, BATCHED, TILES], F32, name="square_sum")
-            square_sum = square_sum_sb[u // BATCHED][:, u % BATCHED, :]
+            batch = batch_of(u)
+            if u == batch[0]:
+                square_sum_sb[u] = small.tile([P, len(batch), TILES], F32, name="square_sum")
+            square_sum = square_sum_sb[batch[0]][:, batch.index(u), :]
             accs = []
             for t in range(TILES):
                 rows = slice(t * P, (t + 1) * P)
@@ -172,37 +183,45 @@ def tile_gep_pa_t_kernel(tc, target_grad, bases0, bases1, bases2, out_0, out_1):
                     func=ACT.Square,
                     accum_out=square_sum[:, t : t + 1],
                 )
-            if u == UNITS - 1:
-                take_roots(u)
+            if len(batch) == 1:
+                take_roots(batch)
             for t in range(TILES):
                 nc.scalar.copy(out=emb[:, t, :], in_=accs[t][:])
             nc.sync.dma_start(out=emb_units[u], in_=emb[:].rearrange("p t j -> p (t j)"))
-            if u % BATCHED == BATCHED - 1 and u != UNITS - 1:
-                take_roots(u)
+            if len(batch) > 1 and u == batch[-1]:
+                take_roots(batch)
 
-        def take_roots(u):
-            norm = small.tile([P, BATCHED, TILES], F32)
-            norm_sb[u // BATCHED] = norm
-            nc.scalar.activation(out=norm[:], in_=square_sum_sb[u // BATCHED][:], func=ACT.Sqrt)
+        def batch_of(u):
+            if u >= UNITS - 2:
+                return [u]
+            return [u - u % 2, u - u % 2 + 1]
+
+        def take_roots(batch):
+            norm = small.tile([P, len(batch), TILES], F32)
+            norm_sb[batch[0]] = norm
+            nc.scalar.activation(out=norm[:], in_=square_sum_sb[batch[0]][:], func=ACT.Sqrt)
 
         def floor_norm(u):
-            if u % BATCHED == BATCHED - 1:
-                floored = small.tile([P, BATCHED, TILES], F32)
-                floored_sb[u // BATCHED] = floored
-                nc.vector.tensor_scalar_max(floored[:], norm_sb[u // BATCHED][:], CLIP)
+            batch = batch_of(u)
+            if u == batch[-1]:
+                floored = small.tile([P, len(batch), TILES], F32)
+                floored_sb[batch[0]] = floored
+                nc.vector.tensor_scalar_max(floored[:], norm_sb[batch[0]][:], CLIP)
 
         def clip_factor(u):
-            if u % BATCHED == BATCHED - 1:
-                factor = small.tile([P, BATCHED, TILES], F32)
-                factor_sb[u // BATCHED] = factor
-                nc.vector.reciprocal(out=factor[:], in_=floored_sb[u // BATCHED][:])
+            batch = batch_of(u)
+            if u == batch[-1]:
+                factor = small.tile([P, len(batch), TILES], F32)
+                for place, unit in enumerate(batch):
+                    factor_sb[unit] = factor[:, place, :]
+                nc.vector.reciprocal(out=factor[:], in_=floored_sb[batch[0]][:])
 
         def weigh(u):
-            scaled = stage.tile([P, TILES, EMB_ALL], F32)
+            scaled = scaled_pool.tile([P, TILES, EMB_ALL], F32)
             scaled_sb[u] = scaled
             for t in range(TILES):
                 nc.vector.tensor_scalar_mul(
-                    scaled[:, t, :], emb_sb[u][:, t, :], factor_sb[u // BATCHED][:, u % BATCHED, t : t + 1]
+                    scaled[:, t, :], emb_sb[u][:, t, :], factor_sb[u][:, t : t + 1]
                 )
 
         def add_up(u):
@@ -217,23 +236,35 @@ def tile_gep_pa_t_kernel(tc, target_grad, bases0, bases1, bases2, out_0, out_1):
                         stop=(u == UNITS - 1 and t == TILES - 1 and g == GROUPS - 1),
                     )
 
-        for step in range(UNITS + 5):
-            if step == 1:
-                quantise_bases()
-            if 0 <= step - 1 < UNITS:
+        for step in range(UNITS + 1):
+            if step >= 1:
                 quantise(step - 1)
-            if 0 <= step - 3 < UNITS:
+            if step == 1:
+                regroup_bases()
+                quantise_bases()
+            if step >= 3:
                 floor_norm(step - 3)
             if step < UNITS:
                 flip_and_regroup(step)
-            if 0 <= step - 3 < UNITS:
+            if step >= 3:
                 clip_factor(step - 3)
-            if 0 <= step - 5 < UNITS:
+            if step >= 5:
                 add_up(step - 5)
-            if 0 <= step - 1 < UNITS:
+            if step >= 1:
                 project(step - 1)
-            if 0 <= step - 4 < UNITS:
+            if step >= 4:
                 weigh(step - 4)
+        floor_norm(UNITS - 2)
+        weigh(UNITS - 3)
+        clip_factor(UNITS - 2)
+        add_up(UNITS - 4)
+        add_up(UNITS - 3)
+        weigh(UNITS - 2)
+        add_up(UNITS - 2)
+        floor_norm(UNITS - 1)
+        clip_factor(UNITS - 1)
+        weigh(UNITS - 1)
+        add_up(UNITS - 1)
 
         nc.vector.tensor_reduce(
             out=column_sums[:, 0:GROUPS], in_=weighted[:], axis=AXIS.X, op=ALU.add

from contextlib import ExitStack

import concourse.mybir as mybir
from concourse.masks import make_identity

F32 = mybir.dt.float32
BF16 = mybir.dt.bfloat16
U32 = mybir.dt.uint32
U8 = mybir.dt.uint8
FP8X4 = mybir.dt.float8_e4m3fn_x4
ACT = mybir.ActivationFunctionType
ALU = mybir.AluOpType
AXIS = mybir.AxisListType

P = 128
PACK = 4
HALVES = 2
BATCH = 4096
GROUPS = 3
K_GROUP = P * PACK
EMB = 128
EMB_ALL = GROUPS * EMB
TILES = 2
UNITS = BATCH // (TILES * P)
CLIP = 1.0
WARM_COLUMNS = 512
WARM_MATMULS = 5
SCALAR_BANKS = 7
OF_BANKS = 16

FLOPS = 2 * BATCH * GROUPS * K_GROUP * EMB


def tile_gep_pa_t_kernel(tc, target_grad, bases0, bases1, bases2, out_0, out_1):
    nc = tc.nc
    bases = [bases0, bases1, bases2]

    grad_units = target_grad.rearrange("(u p t) (g k) -> u p t g k", p=P, t=TILES, g=GROUPS)
    emb_units = out_0.rearrange("(u p t) j -> u p (t j)", p=P, t=TILES)

    with ExitStack() as ctx:
        ctx.enter_context(tc.manual_schedule())
        const = ctx.enter_context(tc.tile_pool(name="const", bufs=1))
        grads = ctx.enter_context(tc.tile_pool(name="grads", bufs=UNITS))
        stage = ctx.enter_context(tc.tile_pool(name="stage", bufs=3))
        embs = ctx.enter_context(tc.tile_pool(name="embs", bufs=UNITS))
        scaled_pool = ctx.enter_context(tc.tile_pool(name="scaled_pool", bufs=5))
        small = ctx.enter_context(tc.tile_pool(name="small", bufs=6))
        flipped_psum = ctx.enter_context(tc.psum_pool(name="flipped_psum", bufs=4))
        emb_psum = ctx.enter_context(tc.psum_pool(name="emb_psum", bufs=3))
        mean_psum = ctx.enter_context(tc.psum_pool(name="mean_psum", bufs=1))

        base_rows = const.tile([P, GROUPS, PACK, EMB], BF16)
        grad_sb = []
        for u in range(UNITS):
            if u == 2:
                for g in range(GROUPS):
                    nc.sync.dma_start(
                        out=base_rows[:, g],
                        in_=bases[g].rearrange("(p t) c -> p t c", t=PACK),
                    )
            if u == 0:
                grad = grads.tile([P, GROUPS, TILES, K_GROUP], BF16, tag="grad")
                for g in range(GROUPS):
                    nc.sync.dma_start(out=grad[:, g], in_=grad_units[u, :, :, g])
                grad_sb.append(grad[:].rearrange("p g t k -> p t g k"))
            else:
                grad = grads.tile([P, TILES, GROUPS, K_GROUP], BF16, tag="grad")
                nc.sync.dma_start(out=grad[:], in_=grad_units[u])
                grad_sb.append(grad[:])

        zeros = const.tile([P, WARM_COLUMNS], BF16)
        nc.vector.memset(zeros[:], 0.0)
        warm = emb_psum.tile([P, WARM_COLUMNS], F32, tag="acc")
        for i in range(WARM_MATMULS):
            nc.tensor.matmul(out=warm[:], lhsT=zeros[:, 0:P], rhs=zeros[:], start=True, stop=True)

        identity = const.tile([P, P], F32)
        make_identity(nc, identity[:])
        root = const.tile([P, 1], F32)
        nc.gpsimd.memset(root[:], 1.0)
        nc.scalar.activation(out=root[:], in_=root[:], func=ACT.Sqrt)
        column_sums = const.tile([P, P], F32)
        nc.vector.memset(column_sums[:], 0.0)
        weighted = mean_psum.tile([P, GROUPS, P], F32)

        base_grouped = const.tile([P, GROUPS, EMB, PACK], BF16, align_bytes=64)
        base_columns = base_rows[:].rearrange("p g t c -> p g c t")
        nc.gpsimd.tensor_scalar(
            out=base_grouped[:, 0],
            in0=base_columns[:, 0],
            scalar1=1.0,
            scalar2=0.0,
            op0=ALU.mult,
            op1=ALU.add,
        )

        def regroup_bases():
            nc.scalar.copy(out=base_grouped[:, 1], in_=base_columns[:, 1])
            nc.vector.tensor_copy(out=base_grouped[:, 2], in_=base_columns[:, 2])

        base_codes = const.tile([P, GROUPS, EMB], U32, align_bytes=64)
        base_scales = const.tile([P, GROUPS, EMB], U8, align_bytes=64)

        def quantise_bases():
            for g in range(GROUPS):
                nc.vector.quantize_mx(
                    out=base_codes[:, g, :].bitcast(FP8X4),
                    scales=base_scales[:, g, :],
                    in_=base_grouped[:, g].rearrange("p c t -> p (c t)"),
                )

        grouped_sb = {}
        codes_sb = {}
        scales_sb = {}
        emb_sb = {}
        square_sum_sb = {}
        norm_sb = {}
        floored_sb = {}
        factor_sb = {}
        scaled_sb = {}

        def flip_and_regroup(u):
            grouped = stage.tile([P, GROUPS, TILES * P * PACK], BF16, align_bytes=64)
            grouped_sb[u] = grouped
            for g in range(GROUPS):
                flipped = flipped_psum.tile([P, TILES, HALVES, P], F32)
                for t in range(TILES):
                    words = grad_sb[u][:, t, g, :].bitcast(F32)
                    for h in range(HALVES):
                        nc.tensor.transpose(
                            flipped[:, t, h, :], words[:, h : HALVES * P : HALVES], identity[:]
                        )
                bank = u * GROUPS + g
                to_scalar = (bank * SCALAR_BANKS) % OF_BANKS < SCALAR_BANKS
                copy = nc.scalar.copy if to_scalar else nc.vector.tensor_copy
                copy(
                    out=grouped[:, g, :]
                    .bitcast(F32)
                    .rearrange("p (t b h) -> p t b h", t=TILES, h=HALVES),
                    in_=flipped[:].rearrange("p t h b -> p t b h"),
                )

        def quantise(u):
            codes = stage.tile([P, GROUPS, TILES * P], U32, align_bytes=64)
            scales = stage.tile([P, GROUPS, TILES * P], U8, align_bytes=64)
            codes_sb[u] = codes
            scales_sb[u] = scales
            for groups in (slice(0, 2), slice(2, 3)):
                nc.vector.quantize_mx(
                    out=codes[:, groups, :].rearrange("p g c -> p (g c)").bitcast(FP8X4),
                    scales=scales[:, groups, :].rearrange("p g c -> p (g c)"),
                    in_=grouped_sb[u][:, groups, :].rearrange("p g c -> p (g c)"),
                )

        def project(u):
            emb = embs.tile([P, TILES, EMB_ALL], F32)
            emb_sb[u] = emb
            batch = batch_of(u)
            if u == batch[0]:
                square_sum_sb[u] = small.tile([P, len(batch), TILES], F32, name="square_sum")
            square_sum = square_sum_sb[batch[0]][:, batch.index(u), :]
            accs = []
            for t in range(TILES):
                rows = slice(t * P, (t + 1) * P)
                acc = emb_psum.tile([P, EMB_ALL], F32)
                accs.append(acc)
                for g in range(GROUPS):
                    nc.tensor.matmul_mx(
                        out=acc[:, g * EMB : (g + 1) * EMB],
                        lhsT=codes_sb[u][:, g, rows].bitcast(FP8X4),
                        lhsT_scale=scales_sb[u][:, g, rows],
                        rhs=base_codes[:, g, :].bitcast(FP8X4),
                        rhs_scale=base_scales[:, g, :],
                        start=True,
                        stop=True,
                    )
            for t in range(TILES):
                squares = stage.tile([P, EMB_ALL], F32)
                nc.scalar.activation(
                    out=squares[:],
                    in_=accs[t][:],
                    func=ACT.Square,
                    accum_out=square_sum[:, t : t + 1],
                )
            if len(batch) == 1:
                take_roots(batch)
            for t in range(TILES):
                nc.scalar.copy(out=emb[:, t, :], in_=accs[t][:])
            nc.sync.dma_start(out=emb_units[u], in_=emb[:].rearrange("p t j -> p (t j)"))
            if len(batch) > 1 and u == batch[-1]:
                take_roots(batch)

        def batch_of(u):
            if u >= UNITS - 2:
                return [u]
            return [u - u % 2, u - u % 2 + 1]

        def take_roots(batch):
            norm = small.tile([P, len(batch), TILES], F32)
            norm_sb[batch[0]] = norm
            nc.scalar.activation(out=norm[:], in_=square_sum_sb[batch[0]][:], func=ACT.Sqrt)

        def floor_norm(u):
            batch = batch_of(u)
            if u == batch[-1]:
                floored = small.tile([P, len(batch), TILES], F32)
                floored_sb[batch[0]] = floored
                nc.vector.tensor_scalar_max(floored[:], norm_sb[batch[0]][:], CLIP)

        def clip_factor(u):
            batch = batch_of(u)
            if u == batch[-1]:
                factor = small.tile([P, len(batch), TILES], F32)
                for place, unit in enumerate(batch):
                    factor_sb[unit] = factor[:, place, :]
                nc.vector.reciprocal(out=factor[:], in_=floored_sb[batch[0]][:])

        def weigh(u):
            scaled = scaled_pool.tile([P, TILES, EMB_ALL], F32)
            scaled_sb[u] = scaled
            for t in range(TILES):
                nc.vector.tensor_scalar_mul(
                    scaled[:, t, :], emb_sb[u][:, t, :], factor_sb[u][:, t : t + 1]
                )

        def add_up(u):
            for t in range(TILES):
                for g in range(GROUPS):
                    nc.tensor.matmul(
                        out=weighted[:, g, :],
                        lhsT=scaled_sb[u][:, t, g * EMB : (g + 1) * EMB],
                        rhs=identity[:],
                        is_transpose=True,
                        start=(u == 0 and t == 0 and g == 0),
                        stop=(u == UNITS - 1 and t == TILES - 1 and g == GROUPS - 1),
                    )

        for step in range(UNITS + 1):
            if step >= 1:
                quantise(step - 1)
            if step == 1:
                regroup_bases()
                quantise_bases()
            if step >= 3:
                floor_norm(step - 3)
            if step < UNITS:
                flip_and_regroup(step)
            if step >= 3:
                clip_factor(step - 3)
            if step >= 5:
                add_up(step - 5)
            if step >= 1:
                project(step - 1)
            if step >= 4:
                weigh(step - 4)
        floor_norm(UNITS - 2)
        weigh(UNITS - 3)
        clip_factor(UNITS - 2)
        add_up(UNITS - 4)
        add_up(UNITS - 3)
        weigh(UNITS - 2)
        add_up(UNITS - 2)
        floor_norm(UNITS - 1)
        clip_factor(UNITS - 1)
        weigh(UNITS - 1)
        add_up(UNITS - 1)

        nc.vector.tensor_reduce(
            out=column_sums[:, 0:GROUPS], in_=weighted[:], axis=AXIS.X, op=ALU.add
        )
        sums_flipped = flipped_psum.tile([P, TILES, HALVES, P], F32, tag="flipped")
        nc.tensor.transpose(sums_flipped[:, 0, 0, :], column_sums[:], identity[:])
        avg = const.tile([P, EMB], F32)
        nc.scalar.activation(
            out=avg[:], in_=sums_flipped[:, 0, 0, :], func=ACT.Copy, scale=CLIP / BATCH
        )
        nc.scalar.dma_start(
            out=out_1.rearrange("(g j) -> g j", g=GROUPS), in_=avg[0:GROUPS, :]
        )
